import numpy as np
import ml_dtypes

BF16 = ml_dtypes.bfloat16


def bf(x):
    return np.asarray(x, np.float32).astype(BF16)


def f32(x):
    return np.asarray(x, np.float32)


def f64(x):
    return np.asarray(x).astype(np.float64)


def striped(idx):
    return np.tile(idx.reshape(-1, 16).T, (8, 1))


C, S, T, N, H, K = 512, 256, 128, 1024, 128, 8


def setup_inputs():
    kv = f32(np.random.standard_normal((C, S)))
    times = f32(np.random.uniform(0.0, 1.0, (1, N)))
    freq = np.random.uniform(-1.5, 1.5, (T, 1))
    phase = np.random.uniform(-1.5, 1.5, (T, 1))
    freq[0, 0] = 1.0 + np.abs(freq[0, 0])
    phase[0, 0] = -0.5 - 0.5 * np.abs(phase[0, 0])
    wt = bf(np.random.standard_normal((T, C)) / np.sqrt(T))
    bt = f32(0.1 * np.random.standard_normal((C, 1)))
    idx = np.concatenate([np.random.permutation(S)[:H] for _ in range(K)])
    return {"kv": kv, "times": times, "freq": f32(freq), "phase": f32(phase), "wt": wt, "bt": bt, "offs": striped(idx)}


def reference(kv, times, freq, phase, wt, bt, offs):
    idx = offs[:16].T.reshape(-1)
    arg = f64(freq) * f64(times) + f64(phase)
    enc = np.sin(arg)
    enc[0] = arg[0]
    tkv = f64(wt).T @ enc + f64(bt)
    return f64(kv)[:, idx] + tkv

@@ -1,0 +1,72 @@
+import concourse.mybir as mybir
+
+F32 = mybir.dt.float32
+BF16 = mybir.dt.bfloat16
+U16 = mybir.dt.uint16
+SIN = mybir.ActivationFunctionType.Sin
+IDENTITY = mybir.ActivationFunctionType.Identity
+MULT = mybir.AluOpType.mult
+ADD = mybir.AluOpType.add
+
+P = 128
+C, S, T, N = 512, 256, 128, 1024
+BLOCKS = C // P
+BANK = 512
+PIECE = S
+
+FLOPS = 2 * T * C * N
+
+
+def tile_tgat_layer_kernel(tc, kv, times, freq, phase, wt, bt, offs, out):
+    nc = tc.nc
+    with (
+        tc.tile_pool(name="held", bufs=1) as held,
+        tc.tile_pool(name="work", bufs=4) as work,
+        tc.psum_pool(name="psum", bufs=8) as psum,
+    ):
+        times_all = held.tile([P, N], F32, name="times_all")
+        nc.sync.dma_start(times_all[:], times.rearrange("o n -> (o n)").partition_broadcast(P))
+        offsets = held.tile([P, N // 16], U16, name="offsets")
+        nc.sync.dma_start(offsets[:], offs)
+        freq_col = held.tile([P, 1], F32, name="freq_col")
+        nc.scalar.dma_start(freq_col[:], freq)
+        phase_col = held.tile([P, 1], F32, name="phase_col")
+        nc.scalar.dma_start(phase_col[:], phase)
+        weights = held.tile([P, C], BF16, name="weights")
+        nc.scalar.dma_start(weights[:], wt)
+        bias_cols = held.tile([P, BLOCKS], F32, name="bias_cols")
+        with nc.allow_non_contiguous_dma(reason="512 biases, one to a partition and block"):
+            nc.scalar.dma_start(bias_cols[:], bt.rearrange("(b p) o -> p (b o)", p=P))
+        windows = []
+        for b in range(BLOCKS):
+            window = held.tile([P, S], F32, name=f"window{b}")
+            nc.sync.dma_start(window[:], kv[b * P : (b + 1) * P, :])
+            windows.append(window)
+
+        enc = held.tile([P, N], BF16, name="enc")
+        nc.scalar.activation(enc[:], times_all[:], SIN, bias=phase_col[:], scale=freq_col[:])
+        nc.vector.tensor_scalar(
+            enc[0:1, :], times_all[0:1, :], freq_col[0:1, :], phase_col[0:1, :], MULT, ADD
+        )
+
+        for h in range(N // BANK):
+            for b in range(BLOCKS):
+                product = psum.tile([P, BANK], F32, name="product")
+                nc.tensor.matmul(
+                    product[:],
+                    weights[:, b * P : (b + 1) * P],
+                    enc[:, h * BANK : (h + 1) * BANK],
+                    start=True,
+                    stop=True,
+                )
+                tkv = work.tile([P, BANK], F32, name="tkv")
+                nc.scalar.activation(tkv[:], product[:], IDENTITY, bias=bias_cols[:, b : b + 1])
+                result = work.tile([P, BANK], F32, name="result")
+                for q in range(BANK // PIECE):
+                    here = slice(q * PIECE, (q + 1) * PIECE)
+                    first = h * BANK + q * PIECE
+                    picked = windows[b][:].indirect(offsets[:, first // 16 : (first + PIECE) // 16])
+                    nc.vector.tensor_tensor(result[:, here], picked, tkv[:, here], ADD)
+                    nc.sync.dma_start(
+                        out[b * P : (b + 1) * P, first : first + PIECE], result[:, here]
+                    )

@@ -11,8 +11,8 @@ ADD = mybir.AluOpType.add
 P = 128
 C, S, T, N = 512, 256, 128, 1024
 BLOCKS = C // P
-BANK = 512
 PIECE = S
+PIECES = N // PIECE
 
 FLOPS = 2 * T * C * N
 
@@ -21,13 +21,9 @@ def tile_tgat_layer_kernel(tc, kv, times, freq, phase, wt, bt, offs, out):
     nc = tc.nc
     with (
         tc.tile_pool(name="held", bufs=1) as held,
-        tc.tile_pool(name="work", bufs=4) as work,
+        tc.tile_pool(name="work", bufs=PIECES * BLOCKS) as work,
         tc.psum_pool(name="psum", bufs=8) as psum,
     ):
-        times_all = held.tile([P, N], F32, name="times_all")
-        nc.sync.dma_start(times_all[:], times.rearrange("o n -> (o n)").partition_broadcast(P))
-        offsets = held.tile([P, N // 16], U16, name="offsets")
-        nc.sync.dma_start(offsets[:], offs)
         freq_col = held.tile([P, 1], F32, name="freq_col")
         nc.scalar.dma_start(freq_col[:], freq)
         phase_col = held.tile([P, 1], F32, name="phase_col")
@@ -37,36 +33,47 @@ def tile_tgat_layer_kernel(tc, kv, times, freq, phase, wt, bt, offs, out):
         bias_cols = held.tile([P, BLOCKS], F32, name="bias_cols")
         with nc.allow_non_contiguous_dma(reason="512 biases, one to a partition and block"):
             nc.scalar.dma_start(bias_cols[:], bt.rearrange("(b p) o -> p (b o)", p=P))
+
+        times_row = times.rearrange("o n -> (o n)")
+        times_all = []
+        for k in range(PIECES):
+            times_piece = held.tile([P, PIECE], F32, name=f"times{k}")
+            nc.sync.dma_start(
+                times_piece[:], times_row[k * PIECE : (k + 1) * PIECE].partition_broadcast(P)
+            )
+            times_all.append(times_piece)
+        offsets = held.tile([P, N // 16], U16, name="offsets")
+        nc.sync.dma_start(offsets[:], offs)
         windows = []
         for b in range(BLOCKS):
             window = held.tile([P, S], F32, name=f"window{b}")
             nc.sync.dma_start(window[:], kv[b * P : (b + 1) * P, :])
             windows.append(window)
 
-        enc = held.tile([P, N], BF16, name="enc")
-        nc.scalar.activation(enc[:], times_all[:], SIN, bias=phase_col[:], scale=freq_col[:])
-        nc.vector.tensor_scalar(
-            enc[0:1, :], times_all[0:1, :], freq_col[0:1, :], phase_col[0:1, :], MULT, ADD
-        )
+        scratch = held.tile([P, 1], F32, name="scratch")
+        nc.vector.memset(scratch[:], 0.0)
+        nc.scalar.activation(scratch[:], scratch[:], SIN)
 
-        for h in range(N // BANK):
+        def encode(k):
+            enc = held.tile([P, PIECE], BF16, name=f"enc{k}")
+            nc.scalar.activation(enc[:], times_all[k][:], SIN, bias=phase_col[:], scale=freq_col[:])
+            nc.gpsimd.tensor_scalar(
+                enc[0:1, :], times_all[k][0:1, :], freq_col[0:1, :], phase_col[0:1, :], MULT, ADD
+            )
+            return enc
+
+        enc_next = encode(0)
+        for k in range(PIECES):
+            enc = enc_next
+            if k + 1 < PIECES:
+                enc_next = encode(k + 1)
+            first = k * PIECE
+            piece_offsets = offsets[:, first // 16 : (first + PIECE) // 16]
             for b in range(BLOCKS):
-                product = psum.tile([P, BANK], F32, name="product")
-                nc.tensor.matmul(
-                    product[:],
-                    weights[:, b * P : (b + 1) * P],
-                    enc[:, h * BANK : (h + 1) * BANK],
-                    start=True,
-                    stop=True,
-                )
-                tkv = work.tile([P, BANK], F32, name="tkv")
+                product = psum.tile([P, PIECE], F32, name="product")
+                nc.tensor.matmul(product[:], weights[:, b * P : (b + 1) * P], enc[:], start=True, stop=True)
+                tkv = work.tile([P, PIECE], F32, name="tkv")
                 nc.scalar.activation(tkv[:], product[:], IDENTITY, bias=bias_cols[:, b : b + 1])
-                result = work.tile([P, BANK], F32, name="result")
-                for q in range(BANK // PIECE):
-                    here = slice(q * PIECE, (q + 1) * PIECE)
-                    first = h * BANK + q * PIECE
-                    picked = windows[b][:].indirect(offsets[:, first // 16 : (first + PIECE) // 16])
-                    nc.vector.tensor_tensor(result[:, here], picked, tkv[:, here], ADD)
-                    nc.sync.dma_start(
-                        out[b * P : (b + 1) * P, first : first + PIECE], result[:, here]
-                    )
+                result = work.tile([P, PIECE], F32, name="result")
+                nc.vector.tensor_tensor(result[:], windows[b][:].indirect(piece_offsets), tkv[:], ADD)
+                nc.sync.dma_start(out[b * P : (b + 1) * P, first : first + PIECE], result[:])

@@ -19,6 +19,8 @@ FLOPS = 2 * T * C * N
 
 def tile_tgat_layer_kernel(tc, kv, times, freq, phase, wt, bt, offs, out):
     nc = tc.nc
+    kv_blocks = kv.rearrange("(p b) s -> b p s", b=BLOCKS)
+    out_blocks = out.rearrange("(p b) n -> b p n", b=BLOCKS)
     with (
         tc.tile_pool(name="held", bufs=1) as held,
         tc.tile_pool(name="work", bufs=PIECES * BLOCKS) as work,
@@ -27,12 +29,12 @@ def tile_tgat_layer_kernel(tc, kv, times, freq, phase, wt, bt, offs, out):
         freq_col = held.tile([P, 1], F32, name="freq_col")
         nc.scalar.dma_start(freq_col[:], freq)
         phase_col = held.tile([P, 1], F32, name="phase_col")
-        nc.scalar.dma_start(phase_col[:], phase)
+        nc.sync.dma_start(phase_col[:], phase)
         weights = held.tile([P, C], BF16, name="weights")
         nc.scalar.dma_start(weights[:], wt)
+        weights_blocks = weights[:].rearrange("u (p b) -> u b p", b=BLOCKS)
         bias_cols = held.tile([P, BLOCKS], F32, name="bias_cols")
-        with nc.allow_non_contiguous_dma(reason="512 biases, one to a partition and block"):
-            nc.scalar.dma_start(bias_cols[:], bt.rearrange("(b p) o -> p (b o)", p=P))
+        nc.scalar.dma_start(bias_cols[:], bt.rearrange("(p b) o -> p (b o)", b=BLOCKS))
 
         times_row = times.rearrange("o n -> (o n)")
         times_all = []
@@ -47,7 +49,7 @@ def tile_tgat_layer_kernel(tc, kv, times, freq, phase, wt, bt, offs, out):
         windows = []
         for b in range(BLOCKS):
             window = held.tile([P, S], F32, name=f"window{b}")
-            nc.sync.dma_start(window[:], kv[b * P : (b + 1) * P, :])
+            nc.sync.dma_start(window[:], kv_blocks[b])
             windows.append(window)
 
         scratch = held.tile([P, 1], F32, name="scratch")
@@ -71,9 +73,9 @@ def tile_tgat_layer_kernel(tc, kv, times, freq, phase, wt, bt, offs, out):
             piece_offsets = offsets[:, first // 16 : (first + PIECE) // 16]
             for b in range(BLOCKS):
                 product = psum.tile([P, PIECE], F32, name="product")
-                nc.tensor.matmul(product[:], weights[:, b * P : (b + 1) * P], enc[:], start=True, stop=True)
+                nc.tensor.matmul(product[:], weights_blocks[:, b, :], enc[:], start=True, stop=True)
                 tkv = work.tile([P, PIECE], F32, name="tkv")
                 nc.scalar.activation(tkv[:], product[:], IDENTITY, bias=bias_cols[:, b : b + 1])
                 result = work.tile([P, PIECE], F32, name="result")
                 nc.vector.tensor_tensor(result[:], windows[b][:].indirect(piece_offsets), tkv[:], ADD)
-                nc.sync.dma_start(out[b * P : (b + 1) * P, first : first + PIECE], result[:])
+                nc.sync.dma_start(out_blocks[b][:, first : first + PIECE], result[:])

@@ -5,7 +5,6 @@ BF16 = mybir.dt.bfloat16
 U16 = mybir.dt.uint16
 SIN = mybir.ActivationFunctionType.Sin
 IDENTITY = mybir.ActivationFunctionType.Identity
-MULT = mybir.AluOpType.mult
 ADD = mybir.AluOpType.add
 
 P = 128
@@ -59,8 +58,8 @@ def tile_tgat_layer_kernel(tc, kv, times, freq, phase, wt, bt, offs, out):
         def encode(k):
             enc = held.tile([P, PIECE], BF16, name=f"enc{k}")
             nc.scalar.activation(enc[:], times_all[k][:], SIN, bias=phase_col[:], scale=freq_col[:])
-            nc.gpsimd.tensor_scalar(
-                enc[0:1, :], times_all[k][0:1, :], freq_col[0:1, :], phase_col[0:1, :], MULT, ADD
+            nc.scalar.activation(
+                enc[0:1, :], times_all[k][0:1, :], IDENTITY, bias=phase_col[0:1, :], scale=freq_col[0:1, :]
             )
             return enc
 

@@ -5,6 +5,7 @@ BF16 = mybir.dt.bfloat16
 U16 = mybir.dt.uint16
 SIN = mybir.ActivationFunctionType.Sin
 IDENTITY = mybir.ActivationFunctionType.Identity
+MULT = mybir.AluOpType.mult
 ADD = mybir.AluOpType.add
 
 P = 128
@@ -28,21 +29,14 @@ def tile_tgat_layer_kernel(tc, kv, times, freq, phase, wt, bt, offs, out):
         freq_col = held.tile([P, 1], F32, name="freq_col")
         nc.scalar.dma_start(freq_col[:], freq)
         phase_col = held.tile([P, 1], F32, name="phase_col")
-        nc.sync.dma_start(phase_col[:], phase)
-        weights = held.tile([P, C], BF16, name="weights")
-        nc.scalar.dma_start(weights[:], wt)
-        weights_blocks = weights[:].rearrange("u (p b) -> u b p", b=BLOCKS)
+        nc.scalar.dma_start(phase_col[:], phase)
         bias_cols = held.tile([P, BLOCKS], F32, name="bias_cols")
         nc.scalar.dma_start(bias_cols[:], bt.rearrange("(p b) o -> p (b o)", b=BLOCKS))
-
-        times_row = times.rearrange("o n -> (o n)")
-        times_all = []
-        for k in range(PIECES):
-            times_piece = held.tile([P, PIECE], F32, name=f"times{k}")
-            nc.sync.dma_start(
-                times_piece[:], times_row[k * PIECE : (k + 1) * PIECE].partition_broadcast(P)
-            )
-            times_all.append(times_piece)
+        times_all = held.tile([P, N], F32, name="times_all")
+        nc.sync.dma_start(times_all[:], times.rearrange("o n -> (o n)").partition_broadcast(P))
+        weights = held.tile([P, C], BF16, name="weights")
+        nc.sync.dma_start(weights[:], wt)
+        weights_blocks = weights[:].rearrange("u (p b) -> u b p", b=BLOCKS)
         offsets = held.tile([P, N // 16], U16, name="offsets")
         nc.sync.dma_start(offsets[:], offs)
         windows = []
@@ -55,26 +49,24 @@ def tile_tgat_layer_kernel(tc, kv, times, freq, phase, wt, bt, offs, out):
         nc.vector.memset(scratch[:], 0.0)
         nc.scalar.activation(scratch[:], scratch[:], SIN)
 
-        def encode(k):
-            enc = held.tile([P, PIECE], BF16, name=f"enc{k}")
-            nc.scalar.activation(enc[:], times_all[k][:], SIN, bias=phase_col[:], scale=freq_col[:])
-            nc.scalar.activation(
-                enc[0:1, :], times_all[k][0:1, :], IDENTITY, bias=phase_col[0:1, :], scale=freq_col[0:1, :]
-            )
-            return enc
-
-        enc_next = encode(0)
+        encs = []
         for k in range(PIECES):
-            enc = enc_next
-            if k + 1 < PIECES:
-                enc_next = encode(k + 1)
-            first = k * PIECE
-            piece_offsets = offsets[:, first // 16 : (first + PIECE) // 16]
-            for b in range(BLOCKS):
+            here = slice(k * PIECE, (k + 1) * PIECE)
+            enc = held.tile([P, PIECE], BF16, name=f"enc{k}")
+            nc.scalar.activation(enc[:], times_all[:, here], SIN, bias=phase_col[:], scale=freq_col[:])
+            nc.vector.tensor_scalar(
+                enc[0:1, :], times_all[0:1, here], freq_col[0:1, :], phase_col[0:1, :], MULT, ADD
+            )
+            encs.append(enc)
+
+        for b in range(BLOCKS):
+            for k in range(PIECES):
+                first = k * PIECE
                 product = psum.tile([P, PIECE], F32, name="product")
-                nc.tensor.matmul(product[:], weights_blocks[:, b, :], enc[:], start=True, stop=True)
+                nc.tensor.matmul(product[:], weights_blocks[:, b, :], encs[k][:], start=True, stop=True)
                 tkv = work.tile([P, PIECE], F32, name="tkv")
                 nc.scalar.activation(tkv[:], product[:], IDENTITY, bias=bias_cols[:, b : b + 1])
                 result = work.tile([P, PIECE], F32, name="result")
-                nc.vector.tensor_tensor(result[:], windows[b][:].indirect(piece_offsets), tkv[:], ADD)
+                picked = windows[b][:].indirect(offsets[:, first // 16 : (first + PIECE) // 16])
+                nc.vector.tensor_tensor(result[:], picked, tkv[:], ADD)
                 nc.sync.dma_start(out_blocks[b][:, first : first + PIECE], result[:])

@@ -13,6 +13,7 @@ C, S, T, N = 512, 256, 128, 1024
 BLOCKS = C // P
 PIECE = S
 PIECES = N // PIECE
+HALF = PIECE // 2
 
 FLOPS = 2 * T * C * N
 
@@ -26,16 +27,16 @@ def tile_tgat_layer_kernel(tc, kv, times, freq, phase, wt, bt, offs, out):
         tc.tile_pool(name="work", bufs=PIECES * BLOCKS) as work,
         tc.psum_pool(name="psum", bufs=8) as psum,
     ):
-        freq_col = held.tile([P, 1], F32, name="freq_col")
-        nc.scalar.dma_start(freq_col[:], freq)
-        phase_col = held.tile([P, 1], F32, name="phase_col")
-        nc.scalar.dma_start(phase_col[:], phase)
-        bias_cols = held.tile([P, BLOCKS], F32, name="bias_cols")
-        nc.scalar.dma_start(bias_cols[:], bt.rearrange("(p b) o -> p (b o)", b=BLOCKS))
         times_all = held.tile([P, N], F32, name="times_all")
         nc.sync.dma_start(times_all[:], times.rearrange("o n -> (o n)").partition_broadcast(P))
+        freq_col = held.tile([P, 1], F32, name="freq_col")
+        nc.sync.dma_start(freq_col[:], freq)
+        phase_col = held.tile([P, 1], F32, name="phase_col")
+        nc.sync.dma_start(phase_col[:], phase)
         weights = held.tile([P, C], BF16, name="weights")
         nc.sync.dma_start(weights[:], wt)
+        bias_cols = held.tile([P, BLOCKS], F32, name="bias_cols")
+        nc.sync.dma_start(bias_cols[:], bt.rearrange("(p b) o -> p (b o)", b=BLOCKS))
         weights_blocks = weights[:].rearrange("u (p b) -> u b p", b=BLOCKS)
         offsets = held.tile([P, N // 16], U16, name="offsets")
         nc.sync.dma_start(offsets[:], offs)
@@ -50,9 +51,9 @@ def tile_tgat_layer_kernel(tc, kv, times, freq, phase, wt, bt, offs, out):
         nc.scalar.activation(scratch[:], scratch[:], SIN)
 
         encs = []
-        for k in range(PIECES):
-            here = slice(k * PIECE, (k + 1) * PIECE)
-            enc = held.tile([P, PIECE], BF16, name=f"enc{k}")
+        for h in range(N // HALF):
+            here = slice(h * HALF, (h + 1) * HALF)
+            enc = held.tile([P, HALF], BF16, name=f"enc{h}")
             nc.scalar.activation(enc[:], times_all[:, here], SIN, bias=phase_col[:], scale=freq_col[:])
             nc.vector.tensor_scalar(
                 enc[0:1, :], times_all[0:1, here], freq_col[0:1, :], phase_col[0:1, :], MULT, ADD
@@ -62,10 +63,14 @@ def tile_tgat_layer_kernel(tc, kv, times, freq, phase, wt, bt, offs, out):
         for b in range(BLOCKS):
             for k in range(PIECES):
                 first = k * PIECE
-                product = psum.tile([P, PIECE], F32, name="product")
-                nc.tensor.matmul(product[:], weights_blocks[:, b, :], encs[k][:], start=True, stop=True)
                 tkv = work.tile([P, PIECE], F32, name="tkv")
-                nc.scalar.activation(tkv[:], product[:], IDENTITY, bias=bias_cols[:, b : b + 1])
+                for half in range(PIECE // HALF):
+                    product = psum.tile([P, HALF], F32, name="product")
+                    enc = encs[first // HALF + half]
+                    nc.tensor.matmul(product[:], weights_blocks[:, b, :], enc[:], start=True, stop=True)
+                    nc.scalar.activation(
+                        tkv[:, half * HALF : (half + 1) * HALF], product[:], IDENTITY, bias=bias_cols[:, b : b + 1]
+                    )
                 result = work.tile([P, PIECE], F32, name="result")
                 picked = windows[b][:].indirect(offsets[:, first // 16 : (first + PIECE) // 16])
                 nc.vector.tensor_tensor(result[:], picked, tkv[:], ADD)

@@ -25,12 +25,12 @@ def tile_tgat_layer_kernel(tc, kv, times, freq, phase, wt, bt, offs, out):
     with (
         tc.tile_pool(name="held", bufs=1) as held,
         tc.tile_pool(name="work", bufs=PIECES * BLOCKS) as work,
-        tc.psum_pool(name="psum", bufs=8) as psum,
+        tc.psum_pool(name="psum", bufs=4) as psum,
     ):
-        times_all = held.tile([P, N], F32, name="times_all")
-        nc.sync.dma_start(times_all[:], times.rearrange("o n -> (o n)").partition_broadcast(P))
-        freq_col = held.tile([P, 1], F32, name="freq_col")
-        nc.sync.dma_start(freq_col[:], freq)
+        times_row = held.tile([1, N], F32, name="times_row")
+        nc.sync.dma_start(times_row[:], times)
+        freq_row = held.tile([1, T], F32, name="freq_row")
+        nc.sync.dma_start(freq_row[:], freq.rearrange("u o -> o u"))
         phase_col = held.tile([P, 1], F32, name="phase_col")
         nc.sync.dma_start(phase_col[:], phase)
         weights = held.tile([P, C], BF16, name="weights")
@@ -53,11 +53,11 @@ def tile_tgat_layer_kernel(tc, kv, times, freq, phase, wt, bt, offs, out):
         encs = []
         for h in range(N // HALF):
             here = slice(h * HALF, (h + 1) * HALF)
+            turns = psum.tile([P, HALF], F32, name="turns")
+            nc.tensor.matmul(turns[:], freq_row[:], times_row[:, here], start=True, stop=True)
             enc = held.tile([P, HALF], BF16, name=f"enc{h}")
-            nc.scalar.activation(enc[:], times_all[:, here], SIN, bias=phase_col[:], scale=freq_col[:])
-            nc.vector.tensor_scalar(
-                enc[0:1, :], times_all[0:1, here], freq_col[0:1, :], phase_col[0:1, :], MULT, ADD
-            )
+            nc.scalar.activation(enc[:], turns[:], SIN, bias=phase_col[:])
+            nc.vector.tensor_scalar(enc[0:1, :], turns[0:1, :], phase_col[0:1, :], None, ADD)
             encs.append(enc)
 
         for b in range(BLOCKS):

@@ -25,14 +25,15 @@ def tile_tgat_layer_kernel(tc, kv, times, freq, phase, wt, bt, offs, out):
     with (
         tc.tile_pool(name="held", bufs=1) as held,
         tc.tile_pool(name="work", bufs=PIECES * BLOCKS) as work,
-        tc.psum_pool(name="psum", bufs=4) as psum,
+        tc.psum_pool(name="psum_angle", bufs=2) as psum_angle,
+        tc.psum_pool(name="psum", bufs=6) as psum,
     ):
-        times_row = held.tile([1, N], F32, name="times_row")
-        nc.sync.dma_start(times_row[:], times)
-        freq_row = held.tile([1, T], F32, name="freq_row")
-        nc.sync.dma_start(freq_row[:], freq.rearrange("u o -> o u"))
-        phase_col = held.tile([P, 1], F32, name="phase_col")
-        nc.sync.dma_start(phase_col[:], phase)
+        ones_times = held.tile([2, N], F32, name="ones_times")
+        nc.sync.dma_start(ones_times[1:2, :], times)
+        nc.vector.memset(ones_times[0:1, :], 1.0)
+        phase_freq = held.tile([2, T], F32, name="phase_freq")
+        nc.sync.dma_start(phase_freq[1:2, :], freq.rearrange("u o -> o u"))
+        nc.sync.dma_start(phase_freq[0:1, :], phase.rearrange("u o -> o u"))
         weights = held.tile([P, C], BF16, name="weights")
         nc.sync.dma_start(weights[:], wt)
         bias_cols = held.tile([P, BLOCKS], F32, name="bias_cols")
@@ -50,27 +51,23 @@ def tile_tgat_layer_kernel(tc, kv, times, freq, phase, wt, bt, offs, out):
         nc.vector.memset(scratch[:], 0.0)
         nc.scalar.activation(scratch[:], scratch[:], SIN)
 
-        encs = []
-        for h in range(N // HALF):
-            here = slice(h * HALF, (h + 1) * HALF)
-            turns = psum.tile([P, HALF], F32, name="turns")
-            nc.tensor.matmul(turns[:], freq_row[:], times_row[:, here], start=True, stop=True)
-            enc = held.tile([P, HALF], BF16, name=f"enc{h}")
-            nc.scalar.activation(enc[:], turns[:], SIN, bias=phase_col[:])
-            nc.vector.tensor_scalar(enc[0:1, :], turns[0:1, :], phase_col[0:1, :], None, ADD)
-            encs.append(enc)
-
-        for b in range(BLOCKS):
-            for k in range(PIECES):
-                first = k * PIECE
+        for k in range(PIECES):
+            first = k * PIECE
+            enc = held.tile([P, PIECE], BF16, name=f"enc{k}")
+            for half in range(PIECE // HALF):
+                here = slice(half * HALF, (half + 1) * HALF)
+                angle = psum_angle.tile([P, HALF], F32, name="angle")
+                nc.tensor.matmul(
+                    angle[:], phase_freq[:], ones_times[:, first + half * HALF : first + (half + 1) * HALF],
+                    start=True, stop=True,
+                )
+                nc.scalar.activation(enc[:, here], angle[:], SIN)
+                nc.scalar.activation(enc[0:1, here], angle[0:1, :], IDENTITY)
+            for b in range(BLOCKS):
+                product = psum.tile([P, PIECE], F32, name="product")
+                nc.tensor.matmul(product[:], weights_blocks[:, b, :], enc[:], start=True, stop=True)
                 tkv = work.tile([P, PIECE], F32, name="tkv")
-                for half in range(PIECE // HALF):
-                    product = psum.tile([P, HALF], F32, name="product")
-                    enc = encs[first // HALF + half]
-                    nc.tensor.matmul(product[:], weights_blocks[:, b, :], enc[:], start=True, stop=True)
-                    nc.scalar.activation(
-                        tkv[:, half * HALF : (half + 1) * HALF], product[:], IDENTITY, bias=bias_cols[:, b : b + 1]
-                    )
+                nc.scalar.activation(tkv[:], product[:], IDENTITY, bias=bias_cols[:, b : b + 1])
                 result = work.tile([P, PIECE], F32, name="result")
                 picked = windows[b][:].indirect(offsets[:, first // 16 : (first + PIECE) // 16])
                 nc.vector.tensor_tensor(result[:], picked, tkv[:], ADD)

@@ -5,7 +5,6 @@ BF16 = mybir.dt.bfloat16
 U16 = mybir.dt.uint16
 SIN = mybir.ActivationFunctionType.Sin
 IDENTITY = mybir.ActivationFunctionType.Identity
-MULT = mybir.AluOpType.mult
 ADD = mybir.AluOpType.add
 
 P = 128
@@ -14,6 +13,8 @@ BLOCKS = C // P
 PIECE = S
 PIECES = N // PIECE
 HALF = PIECE // 2
+
+SHRINK = 2.0**-13
 
 FLOPS = 2 * T * C * N
 
@@ -36,6 +37,7 @@ def tile_tgat_layer_kernel(tc, kv, times, freq, phase, wt, bt, offs, out):
         nc.sync.dma_start(phase_freq[0:1, :], phase.rearrange("u o -> o u"))
         weights = held.tile([P, C], BF16, name="weights")
         nc.sync.dma_start(weights[:], wt)
+        nc.vector.tensor_scalar_mul(weights[0:1, :], weights[0:1, :], 1.0 / SHRINK)
         bias_cols = held.tile([P, BLOCKS], F32, name="bias_cols")
         nc.sync.dma_start(bias_cols[:], bt.rearrange("(p b) o -> p (b o)", b=BLOCKS))
         weights_blocks = weights[:].rearrange("u (p b) -> u b p", b=BLOCKS)
@@ -50,6 +52,9 @@ def tile_tgat_layer_kernel(tc, kv, times, freq, phase, wt, bt, offs, out):
         scratch = held.tile([P, 1], F32, name="scratch")
         nc.vector.memset(scratch[:], 0.0)
         nc.scalar.activation(scratch[:], scratch[:], SIN)
+        sin_scale = held.tile([P, 1], F32, name="sin_scale")
+        nc.vector.memset(sin_scale[:], 1.0)
+        nc.vector.memset(sin_scale[0:1, :], SHRINK)
 
         for k in range(PIECES):
             first = k * PIECE
@@ -61,8 +66,7 @@ def tile_tgat_layer_kernel(tc, kv, times, freq, phase, wt, bt, offs, out):
                     angle[:], phase_freq[:], ones_times[:, first + half * HALF : first + (half + 1) * HALF],
                     start=True, stop=True,
                 )
-                nc.scalar.activation(enc[:, here], angle[:], SIN)
-                nc.scalar.activation(enc[0:1, here], angle[0:1, :], IDENTITY)
+                nc.scalar.activation(enc[:, here], angle[:], SIN, scale=sin_scale[:])
             for b in range(BLOCKS):
                 product = psum.tile([P, PIECE], F32, name="product")
                 nc.tensor.matmul(product[:], weights_blocks[:, b, :], enc[:], start=True, stop=True)

@@ -29,12 +29,13 @@ def tile_tgat_layer_kernel(tc, kv, times, freq, phase, wt, bt, offs, out):
         tc.psum_pool(name="psum_angle", bufs=2) as psum_angle,
         tc.psum_pool(name="psum", bufs=6) as psum,
     ):
-        ones_times = held.tile([2, N], F32, name="ones_times")
-        nc.sync.dma_start(ones_times[1:2, :], times)
-        nc.vector.memset(ones_times[0:1, :], 1.0)
-        phase_freq = held.tile([2, T], F32, name="phase_freq")
-        nc.sync.dma_start(phase_freq[1:2, :], freq.rearrange("u o -> o u"))
-        nc.sync.dma_start(phase_freq[0:1, :], phase.rearrange("u o -> o u"))
+        ones_times = held.tile([P, N], F32, name="ones_times")
+        nc.sync.dma_start(ones_times[P - 1 : P, :], times)
+        nc.vector.memset(ones_times[: P - 1, :], 1.0)
+        phase_freq = held.tile([P, T], F32, name="phase_freq")
+        nc.sync.dma_start(phase_freq[P - 1 : P, :], freq.rearrange("u o -> o u"))
+        nc.sync.dma_start(phase_freq[P - 2 : P - 1, :], phase.rearrange("u o -> o u"))
+        nc.vector.memset(phase_freq[: P - 2, :], 0.0)
         weights = held.tile([P, C], BF16, name="weights")
         nc.sync.dma_start(weights[:], wt)
         nc.vector.tensor_scalar_mul(weights[0:1, :], weights[0:1, :], 1.0 / SHRINK)

@@ -60,19 +60,24 @@ def tile_tgat_layer_kernel(tc, kv, times, freq, phase, wt, bt, offs, out):
         for k in range(PIECES):
             first = k * PIECE
             enc = held.tile([P, PIECE], BF16, name=f"enc{k}")
-            for half in range(PIECE // HALF):
-                here = slice(half * HALF, (half + 1) * HALF)
-                angle = psum_angle.tile([P, HALF], F32, name="angle")
+            chunk = HALF if k == 0 else PIECE
+            for at in range(0, PIECE, chunk):
+                angle = psum_angle.tile([P, chunk], F32, name="angle")
                 nc.tensor.matmul(
-                    angle[:], phase_freq[:], ones_times[:, first + half * HALF : first + (half + 1) * HALF],
-                    start=True, stop=True,
+                    angle[:], phase_freq[:], ones_times[:, first + at : first + at + chunk], start=True, stop=True
                 )
-                nc.scalar.activation(enc[:, here], angle[:], SIN, scale=sin_scale[:])
+                nc.scalar.activation(enc[:, at : at + chunk], angle[:], SIN, scale=sin_scale[:])
             for b in range(BLOCKS):
-                product = psum.tile([P, PIECE], F32, name="product")
-                nc.tensor.matmul(product[:], weights_blocks[:, b, :], enc[:], start=True, stop=True)
                 tkv = work.tile([P, PIECE], F32, name="tkv")
-                nc.scalar.activation(tkv[:], product[:], IDENTITY, bias=bias_cols[:, b : b + 1])
+                chunk = HALF if k == 0 and b == 0 else PIECE
+                for at in range(0, PIECE, chunk):
+                    if k == 0 and b == 0 and at == 0:
+                        product = psum_angle.tile([P, chunk], F32, name="angle")
+                    else:
+                        product = psum.tile([P, chunk], F32, name="product")
+                    here = slice(at, at + chunk)
+                    nc.tensor.matmul(product[:], weights_blocks[:, b, :], enc[:, here], start=True, stop=True)
+                    nc.scalar.activation(tkv[:, here], product[:], IDENTITY, bias=bias_cols[:, b : b + 1])
                 result = work.tile([P, PIECE], F32, name="result")
                 picked = windows[b][:].indirect(offsets[:, first // 16 : (first + PIECE) // 16])
                 nc.vector.tensor_tensor(result[:], picked, tkv[:], ADD)

import concourse.mybir as mybir

F32 = mybir.dt.float32
BF16 = mybir.dt.bfloat16
U16 = mybir.dt.uint16
SIN = mybir.ActivationFunctionType.Sin
IDENTITY = mybir.ActivationFunctionType.Identity
ADD = mybir.AluOpType.add

P = 128
C, S, T, N = 512, 256, 128, 1024
BLOCKS = C // P
PIECE = S
PIECES = N // PIECE
HALF = PIECE // 2

SHRINK = 2.0**-13

FLOPS = 2 * T * C * N


def tile_tgat_layer_kernel(tc, kv, times, freq, phase, wt, bt, offs, out):
    nc = tc.nc
    kv_blocks = kv.rearrange("(p b) s -> b p s", b=BLOCKS)
    out_blocks = out.rearrange("(p b) n -> b p n", b=BLOCKS)
    with (
        tc.tile_pool(name="held", bufs=1) as held,
        tc.tile_pool(name="work", bufs=PIECES * BLOCKS) as work,
        tc.psum_pool(name="psum_angle", bufs=2) as psum_angle,
        tc.psum_pool(name="psum", bufs=6) as psum,
    ):
        ones_times = held.tile([P, N], F32, name="ones_times")
        nc.sync.dma_start(ones_times[P - 1 : P, :], times)
        nc.vector.memset(ones_times[: P - 1, :], 1.0)
        phase_freq = held.tile([P, T], F32, name="phase_freq")
        nc.sync.dma_start(phase_freq[P - 1 : P, :], freq.rearrange("u o -> o u"))
        nc.sync.dma_start(phase_freq[P - 2 : P - 1, :], phase.rearrange("u o -> o u"))
        nc.vector.memset(phase_freq[: P - 2, :], 0.0)
        weights = held.tile([P, C], BF16, name="weights")
        nc.sync.dma_start(weights[:], wt)
        nc.vector.tensor_scalar_mul(weights[0:1, :], weights[0:1, :], 1.0 / SHRINK)
        bias_cols = held.tile([P, BLOCKS], F32, name="bias_cols")
        nc.sync.dma_start(bias_cols[:], bt.rearrange("(p b) o -> p (b o)", b=BLOCKS))
        weights_blocks = weights[:].rearrange("u (p b) -> u b p", b=BLOCKS)
        offsets = held.tile([P, N // 16], U16, name="offsets")
        nc.sync.dma_start(offsets[:], offs)
        windows = []
        for b in range(BLOCKS):
            window = held.tile([P, S], F32, name=f"window{b}")
            nc.sync.dma_start(window[:], kv_blocks[b])
            windows.append(window)

        scratch = held.tile([P, 1], F32, name="scratch")
        nc.vector.memset(scratch[:], 0.0)
        nc.scalar.activation(scratch[:], scratch[:], SIN)
        sin_scale = held.tile([P, 1], F32, name="sin_scale")
        nc.vector.memset(sin_scale[:], 1.0)
        nc.vector.memset(sin_scale[0:1, :], SHRINK)

        for k in range(PIECES):
            first = k * PIECE
            enc = held.tile([P, PIECE], BF16, name=f"enc{k}")
            chunk = HALF if k == 0 else PIECE
            for at in range(0, PIECE, chunk):
                angle = psum_angle.tile([P, chunk], F32, name="angle")
                nc.tensor.matmul(
                    angle[:], phase_freq[:], ones_times[:, first + at : first + at + chunk], start=True, stop=True
                )
                nc.scalar.activation(enc[:, at : at + chunk], angle[:], SIN, scale=sin_scale[:])
            for b in range(BLOCKS):
                tkv = work.tile([P, PIECE], F32, name="tkv")
                chunk = HALF if k == 0 and b == 0 else PIECE
                for at in range(0, PIECE, chunk):
                    if k == 0 and b == 0 and at == 0:
                        product = psum_angle.tile([P, chunk], F32, name="angle")
                    else:
                        product = psum.tile([P, chunk], F32, name="product")
                    here = slice(at, at + chunk)
                    nc.tensor.matmul(product[:], weights_blocks[:, b, :], enc[:, here], start=True, stop=True)
                    nc.scalar.activation(tkv[:, here], product[:], IDENTITY, bias=bias_cols[:, b : b + 1])
                result = work.tile([P, PIECE], F32, name="result")
                picked = windows[b][:].indirect(offsets[:, first // 16 : (first + PIECE) // 16])
                nc.vector.tensor_tensor(result[:], picked, tkv[:], ADD)
                nc.sync.dma_start(out_blocks[b][:, first : first + PIECE], result[:])
